import numpy as np
import ml_dtypes


def mxq(x, axis, fmt="e4m3"):
    dtype, down = {"e4m3": (ml_dtypes.float8_e4m3fn, 7), "e5m2": (ml_dtypes.float8_e5m2, 14)}[fmt]
    v = np.moveaxis(np.asarray(x, np.float32).astype(ml_dtypes.bfloat16).astype(np.float64), axis, -1)
    blocks = v.reshape(v.shape[:-1] + (-1, 32))
    amax = np.abs(blocks).max(-1, keepdims=True)
    byte = np.maximum(np.where(amax > 0, np.frexp(amax)[1] - 1 + 127, 0) - down, 1)
    scale = np.exp2(byte - 127.0)
    codes = (blocks / scale).astype(np.float32).astype(dtype).astype(np.float64)
    return np.moveaxis((codes * scale).reshape(v.shape), -1, axis)


WIDE = False


def mx_kscale(k):
    if not WIDE:
        return np.ones(k)
    levels = np.array([10, -10, 5, -5, 0])
    if k % 512:
        return np.exp2(np.random.permutation(np.resize(levels, k // 32))).repeat(32)
    a = np.empty((k // 512, 16))
    for p in range(k // 512):
        a[p, :8] = np.random.permutation(np.resize(levels, 8))
        for g in range(8):
            far = levels[np.abs(levels - a[p, g]) >= 10]
            a[p, g + 8] = far[np.random.randint(len(far))]
    return np.exp2(a.ravel()).repeat(32)


BF16 = ml_dtypes.bfloat16


def bf(x):
    return np.asarray(x, np.float32).astype(BF16)


def f64(x):
    return np.asarray(x).astype(np.float64)


E2M1 = np.array([0.0, 0.5, 1.0, 1.5, 2.0, 3.0, 4.0, 6.0, -0.0, -0.5, -1.0, -1.5, -2.0, -3.0, -4.0, -6.0])


def pack_weight(w, fmt):
    k, n = w.shape
    w = f64(bf(w)).reshape(k // 32, 32, n)
    amax = np.abs(w).max(1)
    if fmt == "e4m3":
        byte = np.frexp(amax)[1] - 1 + 127 - 7
    else:
        mant, ex = np.frexp(amax / 6.0)
        byte = np.where(mant > 0.5, ex, ex - 1) + 127
    byte = np.clip(np.where(amax > 0, byte, 1), 1, 254)
    scaled = (w * np.exp2(127.0 - byte)[:, None, :]).reshape(k, n).astype(np.float32)
    by_word = np.ascontiguousarray(scaled.reshape(k // 512, 128, 4, n).transpose(0, 1, 3, 2))
    if fmt == "e4m3":
        words = by_word.astype(ml_dtypes.float8_e4m3fn).view(np.uint8)
    else:
        c = by_word.astype(ml_dtypes.float4_e2m1fn).view(np.uint8) & 0xF
        words = c[..., 0::2] | (c[..., 1::2] << 4)
    return np.ascontiguousarray(words), np.ascontiguousarray(byte.astype(np.uint8).reshape(k // 512, 16, n))


def unpack_weight(words, scales, fmt):
    g, p, n, _ = words.shape
    if fmt == "e4m3":
        vals = np.ascontiguousarray(words).view(ml_dtypes.float8_e4m3fn).astype(np.float64)
    else:
        nib = np.empty((g, p, n, 4), np.uint8)
        nib[..., 0::2] = words & 0xF
        nib[..., 1::2] = words >> 4
        vals = E2M1[nib]
    vals = vals * np.repeat(np.exp2(scales.astype(np.float64) - 127.0), 8, axis=1)[..., None]
    return vals.transpose(0, 1, 3, 2).reshape(g * 512, n)


B, EMBED, DETER, STOC, HID, ACT = 4096, 512, 512, 64, 512, 12
DIST = 2 * STOC
CAT = DETER + EMBED


def softplus(v):
    return np.maximum(v, 0.0) + np.log(1.0 + np.exp(-np.abs(v)))


def draw0():
    s = mx_kscale(CAT)
    tp, tq = mx_kscale(HID), mx_kscale(HID)
    r = np.random.standard_normal
    h = bf(r((B, DETER)) * 0.65 * s[:DETER])
    embedding = bf(r((B, EMBED)) * s[DETER:])
    wp1_words, wp1_scales = pack_weight((r((HID, DETER)) / np.sqrt(DETER) / s[:DETER] * tp[:, None]).T, "e4m3")
    bp1 = bf(r(HID) * 0.1 * tp)
    wp2_words, wp2_scales = pack_weight((r((DIST, HID)) / np.sqrt(HID) / tp).T, "e4m3")
    bp2 = bf(r(DIST) * 0.1)
    wq1_words, wq1_scales = pack_weight((r((HID, CAT)) / np.sqrt(CAT) / s * tq[:, None]).T, "e4m3")
    bq1 = bf(r(HID) * 0.1 * tq)
    wq2_words, wq2_scales = pack_weight((r((DIST, HID)) / np.sqrt(HID) / tq).T, "e4m3")
    bq2 = bf(r(DIST) * 0.1)
    return {
        "h": h,
        "embedding": embedding,
        "wp1_words": wp1_words,
        "wp1_scales": wp1_scales,
        "bp1": bp1,
        "wp2_words": wp2_words,
        "wp2_scales": wp2_scales,
        "bp2": bp2,
        "wq1_words": wq1_words,
        "wq1_scales": wq1_scales,
        "bq1": bq1,
        "wq2_words": wq2_words,
        "wq2_scales": wq2_scales,
        "bq2": bq2,
    }


def core(h, embedding, wp1_words, wp1_scales, bp1, wp2_words, wp2_scales, bp2, wq1_words, wq1_scales, bq1, wq2_words, wq2_scales, bq2):
    cq = mxq(np.concatenate([f64(h), f64(embedding)], -1), 1, "e4m3")
    ap = np.maximum((cq[:, :DETER] @ unpack_weight(wp1_words, wp1_scales, "e4m3")) + f64(bp1), 0.0)
    prior = (mxq(ap, 1, "e4m3") @ unpack_weight(wp2_words, wp2_scales, "e4m3")) + f64(bp2)
    prior_mean, prior_std = np.split(prior, 2, axis=-1)
    prior_std = softplus(prior_std) + 0.1
    aq = np.maximum((cq @ unpack_weight(wq1_words, wq1_scales, "e4m3")) + f64(bq1), 0.0)
    post = (mxq(aq, 1, "e4m3") @ unpack_weight(wq2_words, wq2_scales, "e4m3")) + f64(bq2)
    post_mean, post_std = np.split(post, 2, axis=-1)
    post_std = softplus(post_std) + 0.1
    return (post_mean, post_std, prior_mean, prior_std)


def e4m3fn_bytes(y):
    return np.clip(np.asarray(y, np.float64), -448.0, 448.0).astype(np.float32).astype(ml_dtypes.float8_e4m3fn).view(np.uint8)


def e4m3fn_values(b):
    return np.asarray(b, np.uint8).view(ml_dtypes.float8_e4m3fn).astype(np.float64)


def setup_inputs():
    d = draw0()
    x0 = np.asarray(d['h']).astype(np.float64)
    s = (np.max(np.abs(x0), axis=(0,), keepdims=True) / 448.0).astype(np.float32)
    out = {}
    for k, v in d.items():
        if k == 'h':
            out['h_bytes'] = e4m3fn_bytes(x0 / s.astype(np.float64))
            out['h_scale'] = s
        else:
            out[k] = v
    return out


def reference(h_bytes, h_scale, embedding, wp1_words, wp1_scales, bp1, wp2_words, wp2_scales, bp2, wq1_words, wq1_scales, bq1, wq2_words, wq2_scales, bq2):
    return core(e4m3fn_values(h_bytes) * h_scale.astype(np.float64), embedding, wp1_words, wp1_scales, bp1, wp2_words, wp2_scales, bp2, wq1_words, wq1_scales, bq1, wq2_words, wq2_scales, bq2)

@@ -1,0 +1,304 @@
+import math
+from contextlib import ExitStack
+
+import concourse.mybir as mybir
+from concourse.masks import make_identity
+
+B, DETER, EMBED, STOC, HID = 4096, 512, 512, 64, 512
+DIST = 2 * STOC
+FLOPS = 2 * B * (DETER * HID + (DETER + EMBED) * HID + 2 * HID * DIST)
+
+F32 = mybir.dt.float32
+BF16 = mybir.dt.bfloat16
+I32 = mybir.dt.int32
+U32 = mybir.dt.uint32
+U8 = mybir.dt.uint8
+FP8 = mybir.dt.float8_e4m3fn
+FP8X4 = mybir.dt.float8_e4m3fn_x4
+ACT = mybir.ActivationFunctionType
+ALU = mybir.AluOpType
+
+P = 128
+TOK = 512
+NC = B // TOK
+J = 4
+T = 4
+
+LN_SCALE = math.exp(-0.1)
+LN_FLOOR = 2.0**-60
+
+
+def tile_rssmcell_pb_t_w8_kernel(
+    tc, h_bytes, h_scale, embedding, wp1_words, wp1_scales, bp1, wp2_words, wp2_scales, bp2,
+    wq1_words, wq1_scales, bq1, wq2_words, wq2_scales, bq2, out_0, out_1, out_2, out_3,
+):
+    nc = tc.nc
+    h_view = h_bytes.rearrange("(c p j) k -> c p (j k)", p=P, j=J)
+    e_view = embedding.rearrange("(c p j) k -> c p j k", p=P, j=J)
+    mean_views = [o.rearrange("(c p j) d -> c p j d", p=P, j=J) for o in (out_2, out_0)]
+    std_views = [o.rearrange("(c p j) d -> c p j d", p=P, j=J) for o in (out_3, out_1)]
+
+    with ExitStack() as ctx:
+        keep = ctx.enter_context(tc.tile_pool(name="keep", bufs=1))
+        inp = ctx.enter_context(tc.tile_pool(name="inp", bufs=NC))
+        work = ctx.enter_context(tc.tile_pool(name="work", bufs=2))
+        psum_t = ctx.enter_context(tc.psum_pool(name="psum_t", bufs=2))
+        psum_r = ctx.enter_context(tc.psum_pool(name="psum_r", bufs=4))
+        psum_m = ctx.enter_context(tc.psum_pool(name="psum_m", bufs=2))
+
+        ident = keep.tile([P, P], F32, name="ident")
+        scale_row = keep.tile([P, J * DETER], F32, name="scale_row", align_bytes=64)
+        w1_raw = keep.tile([P, 3, HID], I32, name="w1_raw", align_bytes=64)
+        w1 = keep.tile([P, 3, T, P], I32, name="w1", align_bytes=64)
+        w1_sc_raw = keep.tile([P, HID], U8, name="w1_sc_raw", align_bytes=64)
+        w1_sc = keep.tile([P, T, P], U8, name="w1_sc", align_bytes=64)
+        w2 = keep.tile([P, 2, DIST], I32, name="w2", align_bytes=64)
+        w2_sc = keep.tile([P, 2, DIST], U8, name="w2_sc", align_bytes=64)
+        b1_in = keep.tile([P, 2, 32], BF16, name="b1_in", align_bytes=64)
+        b1 = keep.tile([P, 2, T], F32, name="b1", align_bytes=64)
+        b2_in = keep.tile([P, 2, 2, STOC], BF16, name="b2_in", align_bytes=64)
+        b2 = keep.tile([P, 2, 2, STOC], F32, name="b2", align_bytes=64)
+        warm = keep.tile([P, 2], F32, name="warm")
+        dist = keep.tile([P, NC, 2, 2, J, STOC], F32, name="dist", align_bytes=64)
+        std = keep.tile([P, NC, 2, J, STOC], F32, name="std", align_bytes=64)
+
+        h8s = [inp.tile([P, J * DETER], U8, name="h8", align_bytes=64) for c in range(NC)]
+        es = [inp.tile([P, J, EMBED], BF16, name="e", align_bytes=64) for c in range(NC)]
+        hws, hts, ets, planes, groups, codes, scales, banks2 = {}, {}, {}, {}, {}, {}, {}, {}
+
+        def load_e(c):
+            nc.sync.dma_start(out=es[c][:], in_=e_view[c])
+
+        def load_h(c):
+            nc.sync.dma_start(out=h8s[c][:], in_=h_view[c])
+
+        def scale_h(c, lo=0, hi=J * DETER):
+            if lo == 0:
+                hws[c] = work.tile([P, J, DETER], BF16, name="hw", bufs=4, align_bytes=64)
+            nc.vector.tensor_tensor(
+                out=hws[c][:].rearrange("p j k -> p (j k)")[:, lo:hi],
+                in0=h8s[c][:, lo:hi].bitcast(FP8),
+                in1=scale_row[:, 0 : hi - lo],
+                op=ALU.mult,
+            )
+
+        def turn(src, dst):
+            words = src[:].rearrange("p j k -> p (j k)").bitcast(F32).rearrange("p (j w) -> p j w", j=J)
+            out_words = dst[:].rearrange("p n t -> p (n t)").bitcast(F32).rearrange("p (j r u) -> p j r u", r=P, u=2)
+            banks = []
+            for jp in range(2):
+                bank = psum_t.tile([P, 2, 2, P], F32, name="xt")
+                for jj in range(2):
+                    for u in range(2):
+                        nc.tensor.transpose(bank[:, jj, u, :], words[:, 2 * jp + jj, u::2], ident[:])
+                banks.append(bank)
+            for jp in range(2):
+                nc.scalar.copy(out=out_words[:, 2 * jp : 2 * jp + 2], in_=banks[jp][:].rearrange("p j u r -> p j r u"))
+
+        def turn_h(c):
+            hts[c] = work.tile([P, TOK, T], BF16, name="ht", align_bytes=64)
+            turn(hws[c], hts[c])
+
+        def turn_e(c):
+            ets[c] = work.tile([P, TOK, T], BF16, name="et", bufs=3, align_bytes=64)
+            turn(es[c], ets[c])
+
+        def quantize(key, src, bufs, cols=slice(0, TOK)):
+            if cols.start == 0:
+                codes[key] = work.tile([P, TOK], U32, name="codes_" + key[0], bufs=bufs, align_bytes=64)
+                scales[key] = work.tile([P, TOK], U8, name="scales_" + key[0], bufs=bufs, align_bytes=64)
+            nc.vector.quantize_mx(
+                out=codes[key][:, cols].bitcast(FP8X4),
+                scales=scales[key][:, cols],
+                in_=src[:, cols].rearrange("p n t -> p (n t)"),
+            )
+
+        def quantize_h(c):
+            quantize(("h", c), hts[c], 3)
+
+        def quantize_e(c):
+            quantize(("e", c), ets[c], 4)
+
+        def quantize_a(c, head, cols=slice(0, TOK)):
+            quantize(("pq"[head], c), groups[c, head], 2, cols)
+
+        def layer1(c, head, cols=slice(0, TOK)):
+            if cols.start == 0:
+                planes[c, head] = work.tile([P, T, TOK], BF16, name="planes%d" % head, align_bytes=64)
+            passes = [(2, ("h", c))] if head == 0 else [(0, ("h", c)), (1, ("e", c))]
+            for t in range(T):
+                bank = psum_r.tile([P, TOK], F32, name="acc")
+                width = cols.stop - cols.start
+                for k, (slot, key) in enumerate(passes):
+                    nc.tensor.matmul_mx(
+                        out=bank[:, 0:width],
+                        lhsT=w1[:, slot, t, :].bitcast(FP8X4),
+                        lhsT_scale=w1_sc[4 * slot :, t, :],
+                        rhs=codes[key][:, cols].bitcast(FP8X4),
+                        rhs_scale=scales[key][:, cols],
+                        start=(k == 0),
+                        stop=(k == len(passes) - 1),
+                    )
+                nc.scalar.activation(
+                    out=planes[c, head][:, t, cols], in_=bank[:, 0:width], func=ACT.Relu, bias=b1[:, head, t : t + 1]
+                )
+
+        def interleave(c, head, cols=slice(0, TOK)):
+            if cols.start == 0:
+                groups[c, head] = work.tile([P, TOK, T], BF16, name="group%d" % head, align_bytes=64)
+            nc.vector.tensor_copy(
+                out=groups[c, head][:, cols].rearrange("p (n i) t -> p n t i", i=4),
+                in_=planes[c, head][:, :, cols].rearrange("p t (n i) -> p n t i", i=4),
+            )
+
+        def layer2(c, head, js=range(J)):
+            if js.start == 0:
+                banks2[c, head] = psum_m.tile([P, J, DIST], F32, name="dist_acc")
+            key = ("pq"[head], c)
+            for j in js:
+                cols = slice(P * j, P * (j + 1))
+                nc.tensor.matmul_mx(
+                    out=banks2[c, head][:, j, :],
+                    lhsT=codes[key][:, cols].bitcast(FP8X4),
+                    lhsT_scale=scales[key][:, cols],
+                    rhs=w2[:, head, :].bitcast(FP8X4),
+                    rhs_scale=w2_sc[:, head, :],
+                    start=True,
+                    stop=True,
+                )
+
+        def add_bias(c, head, js=range(J)):
+            span = slice(js.start, js.stop)
+            nc.vector.tensor_tensor(
+                out=dist[:, c, head, :, span].rearrange("p s j d -> p j s d"),
+                in0=banks2[c, head][:, span].rearrange("p j (s d) -> p j s d", s=2),
+                in1=b2[:, head].unsqueeze(1).to_broadcast([P, len(js), 2, STOC]),
+                op=ALU.add,
+            )
+            if js.stop == J:
+                nc.sync.dma_start(out=mean_views[head][c], in_=dist[:, c, head, 0])
+
+        def sigmoid(lo, hi, heads=slice(0, 2)):
+            for c in range(lo, hi):
+                nc.scalar.activation(
+                    out=std[:, c, heads].rearrange("p h j d -> p h (j d)"),
+                    in_=dist[:, c, heads, 1].rearrange("p h j d -> p h (j d)"),
+                    func=ACT.Sigmoid, scale=-1.0, bias=0.1,
+                )
+
+        def log(lo, hi):
+            flat = std[:, lo:hi].rearrange("p c h j d -> p (c h j d)")
+            nc.scalar.activation(out=flat, in_=flat, func=ACT.Ln, scale=LN_SCALE, bias=LN_FLOOR)
+
+        def finish(c):
+            flat = std[:, c].rearrange("p h j d -> p h (j d)")
+            nc.vector.scalar_tensor_tensor(
+                out=flat, in0=flat, scalar=-1.0, in1=dist[:, c, :, 1].rearrange("p h j d -> p h (j d)"), op0=ALU.mult, op1=ALU.max
+            )
+            for head in range(2):
+                nc.sync.dma_start(out=std_views[head][c], in_=std[:, c, head])
+
+        make_identity(nc, ident[:])
+        with tc.manual_schedule():
+            nc.gpsimd.memset(warm[:], 0.0)
+            nc.gpsimd.memset(w1_sc_raw[:].bitcast(I32), 0)
+            nc.gpsimd.memset(w2_sc[:].rearrange("p h n -> p (h n)").bitcast(I32), 0)
+            nc.scalar.dma_start(out=scale_row[:, 0:DETER], in_=h_scale.rearrange("o k -> (o k)").partition_broadcast(P))
+            nc.scalar.activation(out=warm[:, 1:2], in_=warm[:, 0:1], func=ACT.Sigmoid)
+            load_h(0)
+            load_e(0)
+            for q in range(4):
+                nc.sync.dma_start(out=w1_sc_raw[32 * q : 32 * q + 8, :].bitcast(I32), in_=wq1_scales[:, 4 * q : 4 * q + 4, :].bitcast(I32))
+                nc.sync.dma_start(out=w1_sc_raw[32 * q + 8 : 32 * q + 12, :].bitcast(I32), in_=wp1_scales[0, 4 * q : 4 * q + 4, :].bitcast(I32))
+            for slot, words in ((2, wp1_words[0]), (0, wq1_words[0]), (1, wq1_words[1])):
+                nc.sync.dma_start(out=w1_raw[:, slot, :], in_=words.rearrange("p n t -> p (n t)").bitcast(I32))
+            for head, b in ((0, bp1), (1, bq1)):
+                nc.scalar.dma_start(out=b1_in[:, head, 0:T], in_=b.rearrange("(p t) -> p t", t=T))
+            load_h(1)
+            load_e(1)
+            for head, (words, sc, b) in enumerate(((wp2_words, wp2_scales, bp2), (wq2_words, wq2_scales, bq2))):
+                nc.sync.dma_start(out=w2[:, head, :], in_=words[0].rearrange("p n t -> p (n t)").bitcast(I32))
+                for q in range(4):
+                    nc.sync.dma_start(out=w2_sc[32 * q : 32 * q + 4, head, :].bitcast(I32), in_=sc[0, 4 * q : 4 * q + 4, :].bitcast(I32))
+                nc.scalar.dma_start(out=b2_in[:, head].rearrange("p s d -> p (s d)"), in_=b.partition_broadcast(P))
+            for c in range(2, NC):
+                load_h(c)
+                load_e(c)
+
+            def permute(slot):
+                nc.vector.tensor_copy(out=w1[:, slot], in_=w1_raw[:, slot, :].rearrange("p (m t) -> p t m", t=T))
+
+            turn_e(0)
+            for j in range(J):
+                scale_h(0, DETER * j, DETER * (j + 1))
+            nc.scalar.copy(out=scale_row[:, 512:1024], in_=scale_row[:, 0:512])
+            nc.scalar.copy(out=scale_row[:, 1024:2048], in_=scale_row[:, 0:1024])
+            quantize_e(0)
+            turn_h(0)
+            permute(2)
+            nc.vector.tensor_copy(out=w1_sc[:], in_=w1_sc_raw[:].rearrange("p (m t) -> p t m", t=T))
+            nc.vector.tensor_copy(out=b1[:], in_=b1_in[:, :, 0:T])
+            quantize_h(0)
+            permute(0)
+            permute(1)
+            turn_e(1)
+            scale_h(1)
+            nc.vector.tensor_copy(out=b2[:, :, 0], in_=b2_in[:, :, 0])
+            nc.vector.tensor_scalar_add(b2[:, :, 1], b2_in[:, :, 1], 0.1)
+            quantize_e(1)
+            scale_h(2)
+
+            left, right = slice(0, TOK // 2), slice(TOK // 2, TOK)
+            last = NC - 1
+            for i in range(NC):
+                prev, nxt = i >= 1, i + 1 < NC
+                if nxt:
+                    turn_h(i + 1)
+                if prev:
+                    interleave(i - 1, 1)
+                    layer2(i - 1, 0)
+                layer1(i, 0)
+                if nxt:
+                    quantize_h(i + 1)
+                if i + 2 < NC:
+                    turn_e(i + 2)
+                if prev:
+                    quantize_a(i - 1, 1)
+                    add_bias(i - 1, 0)
+                    layer2(i - 1, 1)
+                if i + 3 < NC:
+                    scale_h(i + 3)
+                if i >= 2:
+                    sigmoid(i - 2, i - 1)
+                if i == 6:
+                    log(0, 5)
+                    for c in range(5):
+                        finish(c)
+                if i < last:
+                    layer1(i, 1)
+                else:
+                    layer1(i, 1, left)
+                    layer1(i, 1, right)
+                interleave(i, 0)
+                if i + 2 < NC:
+                    quantize_e(i + 2)
+                if prev:
+                    add_bias(i - 1, 1)
+                quantize_a(i, 0)
+            sigmoid(last - 1, last)
+            interleave(last, 1, left)
+            layer2(last, 0)
+            add_bias(last, 0)
+            quantize_a(last, 1, left)
+            sigmoid(last, NC, slice(0, 1))
+            layer2(last, 1, range(0, 2))
+            interleave(last, 1, right)
+            add_bias(last, 1, range(0, 2))
+            quantize_a(last, 1, right)
+            layer2(last, 1, range(2, 4))
+            add_bias(last, 1, range(2, 4))
+            sigmoid(last, NC, slice(1, 2))
+            log(5, 7)
+            log(7, 8)
+            for c in range(5, NC):
+                finish(c)

@@ -56,7 +56,9 @@ def tile_rssmcell_pb_t_w8_kernel(
         w2_sc = keep.tile([P, 2, DIST], U8, name="w2_sc", align_bytes=64)
         b1_in = keep.tile([P, 2, 32], BF16, name="b1_in", align_bytes=64)
         b1 = keep.tile([P, 2, T], F32, name="b1", align_bytes=64)
-        b2_in = keep.tile([P, 2, 2, STOC], BF16, name="b2_in", align_bytes=64)
+        b2_in = keep.tile([P, 2, DIST], BF16, name="b2_in", align_bytes=64)
+        ones = keep.tile([P, P], BF16, name="ones", align_bytes=64)
+        s_col = keep.tile([P, J], F32, name="s_col", align_bytes=64)
         b2 = keep.tile([P, 2, 2, STOC], F32, name="b2", align_bytes=64)
         warm = keep.tile([P, 2], F32, name="warm")
         dist = keep.tile([P, NC, 2, 2, J, STOC], F32, name="dist", align_bytes=64)
@@ -67,7 +69,11 @@ def tile_rssmcell_pb_t_w8_kernel(
         hws, hts, ets, planes, groups, codes, scales, banks2 = {}, {}, {}, {}, {}, {}, {}, {}
 
         def load_e(c):
-            nc.sync.dma_start(out=es[c][:], in_=e_view[c])
+            if c == 0:
+                for jp in range(2):
+                    nc.sync.dma_start(out=es[c][:, 2 * jp : 2 * jp + 2], in_=e_view[c][:, 2 * jp : 2 * jp + 2])
+            else:
+                nc.sync.dma_start(out=es[c][:], in_=e_view[c])
 
         def load_h(c):
             nc.sync.dma_start(out=h8s[c][:], in_=h_view[c])
@@ -198,29 +204,31 @@ def tile_rssmcell_pb_t_w8_kernel(
             for head in range(2):
                 nc.sync.dma_start(out=std_views[head][c], in_=std[:, c, head])
 
-        make_identity(nc, ident[:])
         with tc.manual_schedule():
+            nc.scalar.dma_start(out=s_col[:], in_=h_scale.rearrange("o (p m) -> p (o m)", m=J))
             nc.gpsimd.memset(warm[:], 0.0)
+            make_identity(nc, ident[:])
             nc.gpsimd.memset(w1_sc_raw[:].bitcast(I32), 0)
             nc.gpsimd.memset(w2_sc[:].rearrange("p h n -> p (h n)").bitcast(I32), 0)
-            nc.scalar.dma_start(out=scale_row[:, 0:DETER], in_=h_scale.rearrange("o k -> (o k)").partition_broadcast(P))
+            nc.gpsimd.memset(b2_in[:], 0.0)
+            nc.gpsimd.memset(ones[:], 1.0)
             nc.scalar.activation(out=warm[:, 1:2], in_=warm[:, 0:1], func=ACT.Sigmoid)
-            load_h(0)
             load_e(0)
+            load_h(0)
             for q in range(4):
                 nc.sync.dma_start(out=w1_sc_raw[32 * q : 32 * q + 8, :].bitcast(I32), in_=wq1_scales[:, 4 * q : 4 * q + 4, :].bitcast(I32))
                 nc.sync.dma_start(out=w1_sc_raw[32 * q + 8 : 32 * q + 12, :].bitcast(I32), in_=wp1_scales[0, 4 * q : 4 * q + 4, :].bitcast(I32))
             for slot, words in ((2, wp1_words[0]), (0, wq1_words[0]), (1, wq1_words[1])):
                 nc.sync.dma_start(out=w1_raw[:, slot, :], in_=words.rearrange("p n t -> p (n t)").bitcast(I32))
-            for head, b in ((0, bp1), (1, bq1)):
+            for head, (b, bb) in enumerate(((bp1, bp2), (bq1, bq2))):
                 nc.scalar.dma_start(out=b1_in[:, head, 0:T], in_=b.rearrange("(p t) -> p t", t=T))
+                nc.scalar.dma_start(out=b2_in[0:1, head, :], in_=bb.rearrange("(o n) -> o n", o=1))
             load_h(1)
             load_e(1)
-            for head, (words, sc, b) in enumerate(((wp2_words, wp2_scales, bp2), (wq2_words, wq2_scales, bq2))):
+            for head, (words, sc) in enumerate(((wp2_words, wp2_scales), (wq2_words, wq2_scales))):
                 nc.sync.dma_start(out=w2[:, head, :], in_=words[0].rearrange("p n t -> p (n t)").bitcast(I32))
                 for q in range(4):
                     nc.sync.dma_start(out=w2_sc[32 * q : 32 * q + 4, head, :].bitcast(I32), in_=sc[0, 4 * q : 4 * q + 4, :].bitcast(I32))
-                nc.scalar.dma_start(out=b2_in[:, head].rearrange("p s d -> p (s d)"), in_=b.partition_broadcast(P))
             for c in range(2, NC):
                 load_h(c)
                 load_e(c)
@@ -228,6 +236,12 @@ def tile_rssmcell_pb_t_w8_kernel(
             def permute(slot):
                 nc.vector.tensor_copy(out=w1[:, slot], in_=w1_raw[:, slot, :].rearrange("p (m t) -> p t m", t=T))
 
+            spread = psum_r.tile([P, TOK], F32, name="acc")
+            for m in range(J):
+                nc.tensor.transpose(spread[:, P * m : P * (m + 1)], s_col[:, m : m + 1].to_broadcast([P, P]), ident[:])
+            nc.scalar.copy(
+                out=scale_row[:, 0:DETER].rearrange("p (j m) -> p j m", m=J), in_=spread[:].rearrange("p (m j) -> p j m", m=J)
+            )
             turn_e(0)
             for j in range(J):
                 scale_h(0, DETER * j, DETER * (j + 1))
@@ -243,8 +257,12 @@ def tile_rssmcell_pb_t_w8_kernel(
             permute(1)
             turn_e(1)
             scale_h(1)
-            nc.vector.tensor_copy(out=b2[:, :, 0], in_=b2_in[:, :, 0])
-            nc.vector.tensor_scalar_add(b2[:, :, 1], b2_in[:, :, 1], 0.1)
+            spread2 = psum_m.tile([P, 2, 2, 2, STOC], F32, name="dist_acc")
+            nc.tensor.matmul(
+                spread2[:, 0].rearrange("p h s d -> p (h s d)"), lhsT=ones[:], rhs=b2_in[:].rearrange("p h n -> p (h n)"), start=True, stop=True
+            )
+            nc.vector.tensor_copy(out=b2[:, :, 0], in_=spread2[:, 0, :, 0])
+            nc.vector.tensor_scalar_add(b2[:, :, 1], spread2[:, 0, :, 1], 0.1)
             quantize_e(1)
             scale_h(2)
 
@@ -256,29 +274,26 @@ def tile_rssmcell_pb_t_w8_kernel(
                     turn_h(i + 1)
                 if prev:
                     interleave(i - 1, 1)
-                    layer2(i - 1, 0)
                 layer1(i, 0)
                 if nxt:
                     quantize_h(i + 1)
                 if i + 2 < NC:
                     turn_e(i + 2)
                 if prev:
+                    layer2(i - 1, 0)
                     quantize_a(i - 1, 1)
                     add_bias(i - 1, 0)
-                    layer2(i - 1, 1)
                 if i + 3 < NC:
                     scale_h(i + 3)
                 if i >= 2:
                     sigmoid(i - 2, i - 1)
-                if i == 6:
-                    log(0, 5)
-                    for c in range(5):
-                        finish(c)
                 if i < last:
                     layer1(i, 1)
                 else:
                     layer1(i, 1, left)
                     layer1(i, 1, right)
+                if prev:
+                    layer2(i - 1, 1)
                 interleave(i, 0)
                 if i + 2 < NC:
                     quantize_e(i + 2)
@@ -298,7 +313,6 @@ def tile_rssmcell_pb_t_w8_kernel(
             layer2(last, 1, range(2, 4))
             add_bias(last, 1, range(2, 4))
             sigmoid(last, NC, slice(1, 2))
-            log(5, 7)
-            log(7, 8)
-            for c in range(5, NC):
+            for c in range(0, NC):
+                log(c, c + 1)
                 finish(c)

import math
from contextlib import ExitStack

import concourse.mybir as mybir
from concourse.masks import make_identity

B, DETER, EMBED, STOC, HID = 4096, 512, 512, 64, 512
DIST = 2 * STOC
FLOPS = 2 * B * (DETER * HID + (DETER + EMBED) * HID + 2 * HID * DIST)

F32 = mybir.dt.float32
BF16 = mybir.dt.bfloat16
I32 = mybir.dt.int32
U32 = mybir.dt.uint32
U8 = mybir.dt.uint8
FP8 = mybir.dt.float8_e4m3fn
FP8X4 = mybir.dt.float8_e4m3fn_x4
ACT = mybir.ActivationFunctionType
ALU = mybir.AluOpType

P = 128
TOK = 512
NC = B // TOK
J = 4
T = 4

LN_SCALE = math.exp(-0.1)
LN_FLOOR = 2.0**-60


def tile_rssmcell_pb_t_w8_kernel(
    tc, h_bytes, h_scale, embedding, wp1_words, wp1_scales, bp1, wp2_words, wp2_scales, bp2,
    wq1_words, wq1_scales, bq1, wq2_words, wq2_scales, bq2, out_0, out_1, out_2, out_3,
):
    nc = tc.nc
    h_view = h_bytes.rearrange("(c p j) k -> c p (j k)", p=P, j=J)
    e_view = embedding.rearrange("(c p j) k -> c p j k", p=P, j=J)
    mean_views = [o.rearrange("(c p j) d -> c p j d", p=P, j=J) for o in (out_2, out_0)]
    std_views = [o.rearrange("(c p j) d -> c p j d", p=P, j=J) for o in (out_3, out_1)]

    with ExitStack() as ctx:
        keep = ctx.enter_context(tc.tile_pool(name="keep", bufs=1))
        inp = ctx.enter_context(tc.tile_pool(name="inp", bufs=NC))
        work = ctx.enter_context(tc.tile_pool(name="work", bufs=2))
        psum_t = ctx.enter_context(tc.psum_pool(name="psum_t", bufs=2))
        psum_r = ctx.enter_context(tc.psum_pool(name="psum_r", bufs=4))
        psum_m = ctx.enter_context(tc.psum_pool(name="psum_m", bufs=2))

        ident = keep.tile([P, P], F32, name="ident")
        scale_row = keep.tile([P, J * DETER], F32, name="scale_row", align_bytes=64)
        w1_raw = keep.tile([P, 3, HID], I32, name="w1_raw", align_bytes=64)
        w1 = keep.tile([P, 3, T, P], I32, name="w1", align_bytes=64)
        w1_sc_raw = keep.tile([P, HID], U8, name="w1_sc_raw", align_bytes=64)
        w1_sc = keep.tile([P, T, P], U8, name="w1_sc", align_bytes=64)
        w2 = keep.tile([P, 2, DIST], I32, name="w2", align_bytes=64)
        w2_sc = keep.tile([P, 2, DIST], U8, name="w2_sc", align_bytes=64)
        b1_in = keep.tile([P, 2, 32], BF16, name="b1_in", align_bytes=64)
        b1 = keep.tile([P, 2, T], F32, name="b1", align_bytes=64)
        b2_in = keep.tile([P, 2, DIST], BF16, name="b2_in", align_bytes=64)
        ones = keep.tile([P, P], BF16, name="ones", align_bytes=64)
        s_col = keep.tile([P, J], F32, name="s_col", align_bytes=64)
        b2 = keep.tile([P, 2, 2, STOC], F32, name="b2", align_bytes=64)
        warm = keep.tile([P, 2], F32, name="warm")
        dist = keep.tile([P, NC, 2, 2, J, STOC], F32, name="dist", align_bytes=64)
        std = keep.tile([P, NC, 2, J, STOC], F32, name="std", align_bytes=64)

        h8s = [inp.tile([P, J * DETER], U8, name="h8", align_bytes=64) for c in range(NC)]
        es = [inp.tile([P, J, EMBED], BF16, name="e", align_bytes=64) for c in range(NC)]
        hws, hts, ets, planes, groups, codes, scales, banks2 = {}, {}, {}, {}, {}, {}, {}, {}

        def load_e(c):
            if c == 0:
                for jp in range(2):
                    nc.sync.dma_start(out=es[c][:, 2 * jp : 2 * jp + 2], in_=e_view[c][:, 2 * jp : 2 * jp + 2])
            else:
                nc.sync.dma_start(out=es[c][:], in_=e_view[c])

        def load_h(c):
            nc.sync.dma_start(out=h8s[c][:], in_=h_view[c])

        def scale_h(c, lo=0, hi=J * DETER):
            if lo == 0:
                hws[c] = work.tile([P, J, DETER], BF16, name="hw", bufs=4, align_bytes=64)
            nc.vector.tensor_tensor(
                out=hws[c][:].rearrange("p j k -> p (j k)")[:, lo:hi],
                in0=h8s[c][:, lo:hi].bitcast(FP8),
                in1=scale_row[:, 0 : hi - lo],
                op=ALU.mult,
            )

        def turn(src, dst):
            words = src[:].rearrange("p j k -> p (j k)").bitcast(F32).rearrange("p (j w) -> p j w", j=J)
            out_words = dst[:].rearrange("p n t -> p (n t)").bitcast(F32).rearrange("p (j r u) -> p j r u", r=P, u=2)
            banks = []
            for jp in range(2):
                bank = psum_t.tile([P, 2, 2, P], F32, name="xt")
                for jj in range(2):
                    for u in range(2):
                        nc.tensor.transpose(bank[:, jj, u, :], words[:, 2 * jp + jj, u::2], ident[:])
                banks.append(bank)
            for jp in range(2):
                nc.scalar.copy(out=out_words[:, 2 * jp : 2 * jp + 2], in_=banks[jp][:].rearrange("p j u r -> p j r u"))

        def turn_h(c):
            hts[c] = work.tile([P, TOK, T], BF16, name="ht", align_bytes=64)
            turn(hws[c], hts[c])

        def turn_e(c):
            ets[c] = work.tile([P, TOK, T], BF16, name="et", bufs=3, align_bytes=64)
            turn(es[c], ets[c])

        def quantize(key, src, bufs, cols=slice(0, TOK)):
            if cols.start == 0:
                codes[key] = work.tile([P, TOK], U32, name="codes_" + key[0], bufs=bufs, align_bytes=64)
                scales[key] = work.tile([P, TOK], U8, name="scales_" + key[0], bufs=bufs, align_bytes=64)
            nc.vector.quantize_mx(
                out=codes[key][:, cols].bitcast(FP8X4),
                scales=scales[key][:, cols],
                in_=src[:, cols].rearrange("p n t -> p (n t)"),
            )

        def quantize_h(c):
            quantize(("h", c), hts[c], 3)

        def quantize_e(c):
            quantize(("e", c), ets[c], 4)

        def quantize_a(c, head, cols=slice(0, TOK)):
            quantize(("pq"[head], c), groups[c, head], 2, cols)

        def layer1(c, head, cols=slice(0, TOK)):
            if cols.start == 0:
                planes[c, head] = work.tile([P, T, TOK], BF16, name="planes%d" % head, align_bytes=64)
            passes = [(2, ("h", c))] if head == 0 else [(0, ("h", c)), (1, ("e", c))]
            for t in range(T):
                bank = psum_r.tile([P, TOK], F32, name="acc")
                width = cols.stop - cols.start
                for k, (slot, key) in enumerate(passes):
                    nc.tensor.matmul_mx(
                        out=bank[:, 0:width],
                        lhsT=w1[:, slot, t, :].bitcast(FP8X4),
                        lhsT_scale=w1_sc[4 * slot :, t, :],
                        rhs=codes[key][:, cols].bitcast(FP8X4),
                        rhs_scale=scales[key][:, cols],
                        start=(k == 0),
                        stop=(k == len(passes) - 1),
                    )
                nc.scalar.activation(
                    out=planes[c, head][:, t, cols], in_=bank[:, 0:width], func=ACT.Relu, bias=b1[:, head, t : t + 1]
                )

        def interleave(c, head, cols=slice(0, TOK)):
            if cols.start == 0:
                groups[c, head] = work.tile([P, TOK, T], BF16, name="group%d" % head, align_bytes=64)
            nc.vector.tensor_copy(
                out=groups[c, head][:, cols].rearrange("p (n i) t -> p n t i", i=4),
                in_=planes[c, head][:, :, cols].rearrange("p t (n i) -> p n t i", i=4),
            )

        def layer2(c, head, js=range(J)):
            if js.start == 0:
                banks2[c, head] = psum_m.tile([P, J, DIST], F32, name="dist_acc")
            key = ("pq"[head], c)
            for j in js:
                cols = slice(P * j, P * (j + 1))
                nc.tensor.matmul_mx(
                    out=banks2[c, head][:, j, :],
                    lhsT=codes[key][:, cols].bitcast(FP8X4),
                    lhsT_scale=scales[key][:, cols],
                    rhs=w2[:, head, :].bitcast(FP8X4),
                    rhs_scale=w2_sc[:, head, :],
                    start=True,
                    stop=True,
                )

        def add_bias(c, head, js=range(J)):
            span = slice(js.start, js.stop)
            nc.vector.tensor_tensor(
                out=dist[:, c, head, :, span].rearrange("p s j d -> p j s d"),
                in0=banks2[c, head][:, span].rearrange("p j (s d) -> p j s d", s=2),
                in1=b2[:, head].unsqueeze(1).to_broadcast([P, len(js), 2, STOC]),
                op=ALU.add,
            )
            if js.stop == J:
                nc.sync.dma_start(out=mean_views[head][c], in_=dist[:, c, head, 0])

        def sigmoid(lo, hi, heads=slice(0, 2)):
            for c in range(lo, hi):
                nc.scalar.activation(
                    out=std[:, c, heads].rearrange("p h j d -> p h (j d)"),
                    in_=dist[:, c, heads, 1].rearrange("p h j d -> p h (j d)"),
                    func=ACT.Sigmoid, scale=-1.0, bias=0.1,
                )

        def log(lo, hi):
            flat = std[:, lo:hi].rearrange("p c h j d -> p (c h j d)")
            nc.scalar.activation(out=flat, in_=flat, func=ACT.Ln, scale=LN_SCALE, bias=LN_FLOOR)

        def finish(c):
            flat = std[:, c].rearrange("p h j d -> p h (j d)")
            nc.vector.scalar_tensor_tensor(
                out=flat, in0=flat, scalar=-1.0, in1=dist[:, c, :, 1].rearrange("p h j d -> p h (j d)"), op0=ALU.mult, op1=ALU.max
            )
            for head in range(2):
                nc.sync.dma_start(out=std_views[head][c], in_=std[:, c, head])

        with tc.manual_schedule():
            nc.scalar.dma_start(out=s_col[:], in_=h_scale.rearrange("o (p m) -> p (o m)", m=J))
            nc.gpsimd.memset(warm[:], 0.0)
            make_identity(nc, ident[:])
            nc.gpsimd.memset(w1_sc_raw[:].bitcast(I32), 0)
            nc.gpsimd.memset(w2_sc[:].rearrange("p h n -> p (h n)").bitcast(I32), 0)
            nc.gpsimd.memset(b2_in[:], 0.0)
            nc.gpsimd.memset(ones[:], 1.0)
            nc.scalar.activation(out=warm[:, 1:2], in_=warm[:, 0:1], func=ACT.Sigmoid)
            load_e(0)
            load_h(0)
            for q in range(4):
                nc.sync.dma_start(out=w1_sc_raw[32 * q : 32 * q + 8, :].bitcast(I32), in_=wq1_scales[:, 4 * q : 4 * q + 4, :].bitcast(I32))
                nc.sync.dma_start(out=w1_sc_raw[32 * q + 8 : 32 * q + 12, :].bitcast(I32), in_=wp1_scales[0, 4 * q : 4 * q + 4, :].bitcast(I32))
            for slot, words in ((2, wp1_words[0]), (0, wq1_words[0]), (1, wq1_words[1])):
                nc.sync.dma_start(out=w1_raw[:, slot, :], in_=words.rearrange("p n t -> p (n t)").bitcast(I32))
            for head, (b, bb) in enumerate(((bp1, bp2), (bq1, bq2))):
                nc.scalar.dma_start(out=b1_in[:, head, 0:T], in_=b.rearrange("(p t) -> p t", t=T))
                nc.scalar.dma_start(out=b2_in[0:1, head, :], in_=bb.rearrange("(o n) -> o n", o=1))
            load_h(1)
            load_e(1)
            for head, (words, sc) in enumerate(((wp2_words, wp2_scales), (wq2_words, wq2_scales))):
                nc.sync.dma_start(out=w2[:, head, :], in_=words[0].rearrange("p n t -> p (n t)").bitcast(I32))
                for q in range(4):
                    nc.sync.dma_start(out=w2_sc[32 * q : 32 * q + 4, head, :].bitcast(I32), in_=sc[0, 4 * q : 4 * q + 4, :].bitcast(I32))
            for c in range(2, NC):
                load_h(c)
                load_e(c)

            def permute(slot):
                nc.vector.tensor_copy(out=w1[:, slot], in_=w1_raw[:, slot, :].rearrange("p (m t) -> p t m", t=T))

            spread = psum_r.tile([P, TOK], F32, name="acc")
            for m in range(J):
                nc.tensor.transpose(spread[:, P * m : P * (m + 1)], s_col[:, m : m + 1].to_broadcast([P, P]), ident[:])
            nc.scalar.copy(
                out=scale_row[:, 0:DETER].rearrange("p (j m) -> p j m", m=J), in_=spread[:].rearrange("p (m j) -> p j m", m=J)
            )
            turn_e(0)
            for j in range(J):
                scale_h(0, DETER * j, DETER * (j + 1))
            nc.scalar.copy(out=scale_row[:, 512:1024], in_=scale_row[:, 0:512])
            nc.scalar.copy(out=scale_row[:, 1024:2048], in_=scale_row[:, 0:1024])
            quantize_e(0)
            turn_h(0)
            permute(2)
            nc.vector.tensor_copy(out=w1_sc[:], in_=w1_sc_raw[:].rearrange("p (m t) -> p t m", t=T))
            nc.vector.tensor_copy(out=b1[:], in_=b1_in[:, :, 0:T])
            quantize_h(0)
            permute(0)
            permute(1)
            turn_e(1)
            scale_h(1)
            spread2 = psum_m.tile([P, 2, 2, 2, STOC], F32, name="dist_acc")
            nc.tensor.matmul(
                spread2[:, 0].rearrange("p h s d -> p (h s d)"), lhsT=ones[:], rhs=b2_in[:].rearrange("p h n -> p (h n)"), start=True, stop=True
            )
            nc.vector.tensor_copy(out=b2[:, :, 0], in_=spread2[:, 0, :, 0])
            nc.vector.tensor_scalar_add(b2[:, :, 1], spread2[:, 0, :, 1], 0.1)
            quantize_e(1)
            scale_h(2)

            left, right = slice(0, TOK // 2), slice(TOK // 2, TOK)
            last = NC - 1
            for i in range(NC):
                prev, nxt = i >= 1, i + 1 < NC
                if nxt:
                    turn_h(i + 1)
                if prev:
                    interleave(i - 1, 1)
                layer1(i, 0)
                if nxt:
                    quantize_h(i + 1)
                if i + 2 < NC:
                    turn_e(i + 2)
                if prev:
                    layer2(i - 1, 0)
                    quantize_a(i - 1, 1)
                    add_bias(i - 1, 0)
                if i + 3 < NC:
                    scale_h(i + 3)
                if i >= 2:
                    sigmoid(i - 2, i - 1)
                if i < last:
                    layer1(i, 1)
                else:
                    layer1(i, 1, left)
                    layer1(i, 1, right)
                if prev:
                    layer2(i - 1, 1)
                interleave(i, 0)
                if i + 2 < NC:
                    quantize_e(i + 2)
                if prev:
                    add_bias(i - 1, 1)
                quantize_a(i, 0)
            sigmoid(last - 1, last)
            interleave(last, 1, left)
            layer2(last, 0)
            add_bias(last, 0)
            quantize_a(last, 1, left)
            sigmoid(last, NC, slice(0, 1))
            layer2(last, 1, range(0, 2))
            interleave(last, 1, right)
            add_bias(last, 1, range(0, 2))
            quantize_a(last, 1, right)
            layer2(last, 1, range(2, 4))
            add_bias(last, 1, range(2, 4))
            sigmoid(last, NC, slice(1, 2))
            for c in range(0, NC):
                log(c, c + 1)
                finish(c)
